import numpy as np
import ml_dtypes


def mxq(x, axis, fmt="e4m3"):
    dtype, down = {"e4m3": (ml_dtypes.float8_e4m3fn, 7), "e5m2": (ml_dtypes.float8_e5m2, 14)}[fmt]
    v = np.moveaxis(np.asarray(x, np.float32).astype(ml_dtypes.bfloat16).astype(np.float64), axis, -1)
    blocks = v.reshape(v.shape[:-1] + (-1, 32))
    amax = np.abs(blocks).max(-1, keepdims=True)
    byte = np.maximum(np.where(amax > 0, np.frexp(amax)[1] - 1 + 127, 0) - down, 1)
    scale = np.exp2(byte - 127.0)
    codes = (blocks / scale).astype(np.float32).astype(dtype).astype(np.float64)
    return np.moveaxis((codes * scale).reshape(v.shape), -1, axis)


WIDE = False


def mx_kscale(k):
    if not WIDE:
        return np.ones(k)
    levels = np.array([10, -10, 5, -5, 0])
    a = np.random.permutation(np.resize(levels, k // 512 * 4)).reshape(k // 512, 4)
    idx = np.arange(k)
    return np.exp2(a[idx // 512, idx % 128 // 32])


BF16 = ml_dtypes.bfloat16


def bf(x):
    return np.asarray(x, np.float32).astype(BF16)


def f64(x):
    return np.asarray(x).astype(np.float64)


B, P, WS, D, H = 2, 24, 8, 1024, 16
WN = P // WS
N = WS * WS
SHIFT = WS // 2
LN_EPS = 1e-5


def layer_norm(x, g, b):
    mu = x.mean(-1, keepdims=True)
    var = x.var(-1, keepdims=True)
    return (x - mu) / np.sqrt(var + LN_EPS) * g + b


def window_merge(win):
    x = win.reshape(B, WN, WN, WS, WS, D).transpose(0, 1, 3, 2, 4, 5)
    return x.reshape(B, P, P, D)


def setup_inputs():
    s, t = mx_kscale(D), mx_kscale(D)
    x_mid = np.random.standard_normal((B, P * P, D)) * 1.4 + np.random.standard_normal((B, P * P, 1)) * 0.5
    return {"attn_win": bf(np.random.standard_normal((B * WN * WN, N, D)) * 0.4 * s),
            "x_mid": bf(x_mid),
            "Wo2": bf(np.random.standard_normal((D, D)) / np.sqrt(D) / s[:, None]),
            "bo2": bf(0.1 * np.random.standard_normal(D)),
            "g4": bf((1.0 + 0.1 * np.random.standard_normal(D)) * t),
            "b4": bf(0.1 * np.random.standard_normal(D) * t),
            "Wl": bf(np.random.standard_normal((D, D)) / np.sqrt(D) / t[:, None]),
            "bl": bf(0.1 * np.random.standard_normal(D))}


def reference(attn_win, x_mid, Wo2, bo2, g4, b4, Wl, bl):
    a = (mxq(f64(attn_win), 2, "e4m3") @ mxq(f64(Wo2), 0, "e4m3")) + f64(bo2)
    a = np.roll(window_merge(a), (-SHIFT, -SHIFT), axis=(1, 2)).reshape(B, P * P, D)
    x = f64(x_mid) + a
    h = layer_norm(x, f64(g4), f64(b4))
    return x + (mxq(h, 2, "e4m3") @ mxq(f64(Wl), 0, "e4m3")) + f64(bl)

@@ -1,0 +1,299 @@
+from contextlib import ExitStack
+
+import concourse.mybir as mybir
+from concourse.masks import make_identity
+
+F32 = mybir.dt.float32
+BF16 = mybir.dt.bfloat16
+U32 = mybir.dt.uint32
+U8 = mybir.dt.uint8
+FP8X4 = mybir.dt.float8_e4m3fn_x4
+ALU = mybir.AluOpType
+ACT = mybir.ActivationFunctionType
+
+P = 128
+D = 1024
+PACK = 4
+K_PASS = P * PACK
+PASSES = D // K_PASS
+N_PASS = 512
+HALVES = D // N_PASS
+IMAGES = 2
+SIDE = 24
+WS = 8
+WN = SIDE // WS
+SHIFT = WS // 2
+TOKENS = IMAGES * SIDE * SIDE
+TILES = TOKENS // P
+LN_EPS = 1e-5
+FLOPS = 2 * 2 * TOKENS * D * D
+
+
+def rolled_runs(w):
+    start = WS * w - SHIFT
+    if start < 0:
+        return [(0, SHIFT, start + SIDE), (SHIFT, WS - SHIFT, 0)]
+    return [(0, WS, start)]
+
+
+V_COLS = 320
+
+
+def quantise_weight(nc, stage, raw, codes, scales):
+    for g in range(PASSES):
+        for h in range(HALVES):
+            first = h * N_PASS
+            grouped = stage.tile([P, N_PASS, PACK], BF16, align_bytes=64)
+            nc.vector.tensor_copy(
+                out=grouped[:, 0:V_COLS, :].rearrange("p (c i) t -> p c t i", i=4),
+                in_=raw[:, g * PACK : (g + 1) * PACK, first : first + V_COLS].rearrange("p t (c i) -> p c t i", i=4),
+            )
+            nc.scalar.copy(
+                out=grouped[:, V_COLS:N_PASS, :].rearrange("p (c i) t -> p c t i", i=4),
+                in_=raw[:, g * PACK : (g + 1) * PACK, first + V_COLS : first + N_PASS].rearrange(
+                    "p t (c i) -> p c t i", i=4
+                ),
+            )
+            nc.vector.quantize_mx(
+                out=codes[:, g, first : first + N_PASS].bitcast(FP8X4),
+                scales=scales[:, g, first : first + N_PASS],
+                in_=grouped[:].rearrange("p n t -> p (n t)"),
+            )
+
+
+def tile_successiveswintransfomerblock_pb_kernel(tc, attn_win, x_mid, Wo2, bo2, g4, b4, Wl, bl, out):
+    nc = tc.nc
+    attn_rows = attn_win.flatten_outer_dims()
+    xmid_rows = x_mid.flatten_outer_dims()
+    out_rows = out.flatten_outer_dims()
+
+    with ExitStack() as ctx:
+        keep = ctx.enter_context(tc.tile_pool(name="keep", bufs=1))
+        stage = ctx.enter_context(tc.tile_pool(name="stage", bufs=3))
+        stream = ctx.enter_context(tc.tile_pool(name="stream", bufs=3))
+        short = ctx.enter_context(tc.tile_pool(name="short", bufs=2))
+        small = ctx.enter_context(tc.tile_pool(name="small", bufs=4))
+        psum_mm = ctx.enter_context(tc.psum_pool(name="psum_mm", bufs=2))
+        psum_tr = ctx.enter_context(tc.psum_pool(name="psum_tr", bufs=4))
+
+        vec_rows = keep.tile([P, P], BF16)
+        nc.vector.memset(vec_rows[:], 0.0)
+        nc.scalar.dma_start(out=vec_rows[0:8, :], in_=g4.rearrange("(c p) -> c p", p=P))
+        nc.scalar.dma_start(out=vec_rows[8:16, :], in_=b4.rearrange("(c p) -> c p", p=P))
+        bo2_all = keep.tile([P, D], BF16)
+        nc.scalar.dma_start(out=bo2_all[:], in_=bo2.partition_broadcast(P))
+        bl_all = keep.tile([P, D], BF16)
+        nc.scalar.dma_start(out=bl_all[:], in_=bl.partition_broadcast(P))
+        eps = keep.tile([P, 1], F32)
+        nc.vector.memset(eps[:], LN_EPS)
+        ident = keep.tile([P, P], F32)
+        make_identity(nc, ident[:])
+
+        attn_sb = keep.tile([P, TILES, D], BF16)
+        attn_src = attn_rows.rearrange("(s q) d -> q s d", q=P)
+        xmid_sb = keep.tile([P, TILES, D], BF16)
+        xmid_src = xmid_rows.rearrange("(s q) d -> q s d", q=P)
+        wo_raw = keep.tile([P, PASSES * PACK, D], BF16)
+        wo_dst = wo_raw[:].rearrange("q (c e) n -> q c (e n)", e=2)
+        wo_src = Wo2.rearrange("(c q e) n -> q c (e n)", q=P, e=2)
+        wl_raw = keep.tile([P, PASSES * PACK, D], BF16)
+        wl_src = Wl.rearrange("(c p) n -> p c n", p=P)
+
+        nc.sync.dma_start(out=attn_sb[:, 0:3, :], in_=attn_src[:, 0:3, :])
+        for g in range(PASSES):
+            nc.sync.dma_start(out=wo_dst[:, 2 * g : 2 * g + 2, :], in_=wo_src[:, 2 * g : 2 * g + 2, :])
+        for first in range(3, TILES, 3):
+            nc.sync.dma_start(out=attn_sb[:, first : first + 3, :], in_=attn_src[:, first : first + 3, :])
+        nc.sync.dma_start(out=xmid_sb[:, 0:3, :], in_=xmid_src[:, 0:3, :])
+        for g in range(PASSES):
+            nc.sync.dma_start(
+                out=wl_raw[:, g * PACK : (g + 1) * PACK, :], in_=wl_src[:, g * PACK : (g + 1) * PACK, :]
+            )
+        for first in range(3, TILES, 3):
+            nc.sync.dma_start(out=xmid_sb[:, first : first + 3, :], in_=xmid_src[:, first : first + 3, :])
+
+        wo_codes = keep.tile([P, PASSES, D], U32, align_bytes=64)
+        wo_scales = keep.tile([P, PASSES, D], U8, align_bytes=64)
+        wl_codes = keep.tile([P, PASSES, D], U32, align_bytes=64)
+        wl_scales = keep.tile([P, PASSES, D], U8, align_bytes=64)
+        attn_grouped = keep.tile([P, PASSES, TOKENS, PACK], BF16, align_bytes=64)
+        attn_codes = keep.tile([P, PASSES, TOKENS], U32, align_bytes=64)
+        attn_scales = keep.tile([P, PASSES, TOKENS], U8, align_bytes=64)
+        by_patch = attn_grouped[:].bitcast(F32).rearrange("p g (b r c) u -> p g b r c u", r=SIDE, c=SIDE)
+
+        def flip_attn(s):
+            flipped = psum_tr.tile([P, PASSES * 2, P], F32, tag="tr")
+            for c in range(PASSES * 2):
+                nc.tensor.transpose(flipped[:, c, :], attn_sb[:, s, :].bitcast(F32)[:, c * P : (c + 1) * P], ident[:])
+            by_window = flipped[:].rearrange("p c (w i j) -> p c w i j", i=WS, j=WS)
+            for w in range(2):
+                image, in_image = divmod(2 * s + w, WN * WN)
+                wr, wc = divmod(in_image, WN)
+                for i0, n_rows, r0 in rolled_runs(wr):
+                    for j0, n_cols, c0 in rolled_runs(wc):
+                        for g in range(PASSES):
+                            src = by_window[:, 2 * g : 2 * g + 2, w, i0 : i0 + n_rows, j0 : j0 + n_cols]
+                            dst = by_patch[:, g, image, r0 : r0 + n_rows, c0 : c0 + n_cols, :]
+                            nc.scalar.copy(out=dst, in_=src.rearrange("p u i j -> p i j u"))
+
+        def quantise_attn(i):
+            toks = slice(i * P, (i + 1) * P)
+            for g in range(PASSES):
+                nc.vector.quantize_mx(
+                    out=attn_codes[:, g, toks].bitcast(FP8X4),
+                    scales=attn_scales[:, g, toks],
+                    in_=attn_grouped[:, g, toks, :].rearrange("p n t -> p (n t)"),
+                )
+
+        xb, acc1, x, xbl, negmean, rstd, shift, xn, flipped_xn, planes, h_codes, h_scales, acc2 = (
+            {}, {}, {}, {}, {}, {}, {}, {}, {}, {}, {}, {}, {},
+        )
+
+        def add_bo2(i):
+            xb[i] = stream.tile([P, D], F32, name="xb")
+            nc.gpsimd.tensor_tensor(out=xb[i][:], in0=xmid_sb[:, i, :], in1=bo2_all[:], op=ALU.add)
+
+        def project(i):
+            toks = slice(i * P, (i + 1) * P)
+            for h in range(HALVES):
+                cols = slice(h * N_PASS, (h + 1) * N_PASS)
+                acc1[i, h] = psum_mm.tile([P, N_PASS], F32, name="acc1")
+                for g in range(PASSES):
+                    nc.tensor.matmul_mx(
+                        out=acc1[i, h][:],
+                        lhsT=attn_codes[:, g, toks].bitcast(FP8X4),
+                        lhsT_scale=attn_scales[:, g, toks],
+                        rhs=wo_codes[:, g, cols].bitcast(FP8X4),
+                        rhs_scale=wo_scales[:, g, cols],
+                        start=(g == 0),
+                        stop=(g == PASSES - 1),
+                    )
+
+        def residual(i):
+            x[i] = stream.tile([P, D], F32, name="x")
+            sums = small.tile([P, HALVES], F32)
+            for h in range(HALVES):
+                cols = slice(h * N_PASS, (h + 1) * N_PASS)
+                nc.vector.scalar_tensor_tensor(
+                    out=x[i][:, cols], in0=acc1[i, h][:], scalar=1.0, in1=xb[i][:, cols],
+                    op0=ALU.mult, op1=ALU.add, accum_out=sums[:, h : h + 1],
+                )
+            negmean[i] = small.tile([P, 1], F32, name="negmean")
+            nc.vector.tensor_scalar(
+                out=negmean[i][:], in0=sums[:, 0:1], scalar1=sums[:, 1:2], scalar2=-1.0 / D,
+                op0=ALU.add, op1=ALU.mult,
+            )
+
+        def add_bl(i):
+            xbl[i] = stream.tile([P, D], F32, name="xbl")
+            nc.gpsimd.tensor_tensor(out=xbl[i][:], in0=x[i][:], in1=bl_all[:], op=ALU.add)
+
+        def statistics(i):
+            squares = short.tile([P, D], BF16)
+            ssq = small.tile([P, 1], F32)
+            nc.scalar.activation(
+                out=squares[:], in_=x[i][:], func=ACT.Square, bias=negmean[i][:], scale=1.0, accum_out=ssq[:]
+            )
+            rstd[i] = small.tile([P, 1], F32, name="rstd")
+            nc.scalar.activation(out=rstd[i][:], in_=ssq[:], func=ACT.Abs_reciprocal_sqrt, bias=eps[:], scale=1.0 / D)
+            shift[i] = small.tile([P, 1], F32, name="shift")
+            nc.scalar.activation(out=shift[i][:], in_=negmean[i][:], func=ACT.Identity, scale=rstd[i][:])
+
+        def normalise(i):
+            xn[i] = short.tile([P, D], F32, name="xn")
+            nc.scalar.activation(out=xn[i][:], in_=x[i][:], func=ACT.Identity, bias=shift[i][:], scale=rstd[i][:])
+
+        def flip(i):
+            for g in range(PASSES):
+                flipped_xn[i, g] = psum_tr.tile([P, PACK, P], F32, name="flipped_xn", tag="tr")
+                for t in range(PACK):
+                    c = g * PACK + t
+                    nc.tensor.transpose(flipped_xn[i, g][:, t, :], xn[i][:, c * P : (c + 1) * P], ident[:])
+
+        def gain_and_bias(i):
+            planes[i] = short.tile([P, PASSES * PACK, P], BF16, name="planes")
+            for t in range(PACK):
+                nc.vector.tensor_scalar(
+                    out=planes[i][:, t, :], in0=flipped_xn[i, 0][:, t, :],
+                    scalar1=vec_cols[:, t : t + 1], scalar2=vec_cols[:, 8 + t : 9 + t], op0=ALU.mult, op1=ALU.add,
+                )
+                c = PACK + t
+                nc.scalar.activation(
+                    out=planes[i][:, c, :], in_=flipped_xn[i, 1][:, t, :], func=ACT.Identity,
+                    bias=vec_cols[:, 8 + c : 9 + c], scale=vec_cols[:, c : c + 1],
+                )
+
+        def quantise_h(i):
+            h_grouped = short.tile([P, PASSES, P, PACK], BF16, align_bytes=64)
+            nc.vector.tensor_copy(out=h_grouped[:], in_=planes[i][:].rearrange("p (g t) n -> p g n t", t=PACK))
+            h_codes[i] = short.tile([P, PASSES, P], U32, align_bytes=64, name="h_codes")
+            h_scales[i] = short.tile([P, PASSES, P], U8, align_bytes=64, name="h_scales")
+            nc.vector.quantize_mx(
+                out=h_codes[i][:].rearrange("p g n -> p (g n)").bitcast(FP8X4),
+                scales=h_scales[i][:].rearrange("p g n -> p (g n)"),
+                in_=h_grouped[:].rearrange("p g n t -> p (g n t)"),
+            )
+
+        def linear(i):
+            for h in range(HALVES):
+                cols = slice(h * N_PASS, (h + 1) * N_PASS)
+                acc2[i, h] = psum_mm.tile([P, N_PASS], F32, name="acc2")
+                for g in range(PASSES):
+                    nc.tensor.matmul_mx(
+                        out=acc2[i, h][:],
+                        lhsT=h_codes[i][:, g, :].bitcast(FP8X4),
+                        lhsT_scale=h_scales[i][:, g, :],
+                        rhs=wl_codes[:, g, cols].bitcast(FP8X4),
+                        rhs_scale=wl_scales[:, g, cols],
+                        start=(g == 0),
+                        stop=(g == PASSES - 1),
+                    )
+
+        def finish(i):
+            result = stream.tile([P, D], F32)
+            for h in range(HALVES):
+                cols = slice(h * N_PASS, (h + 1) * N_PASS)
+                nc.vector.tensor_tensor(out=result[:, cols], in0=acc2[i, h][:], in1=xbl[i][:, cols], op=ALU.add)
+            nc.sync.dma_start(out=out_rows[i * P : (i + 1) * P, :], in_=result[:])
+
+        for s in range(3):
+            flip_attn(s)
+        quantise_weight(nc, stage, wo_raw, wo_codes, wo_scales)
+        for s in range(3, TILES):
+            flip_attn(s)
+        for i in range(TILES):
+            quantise_attn(i)
+        add_bo2(0)
+        add_bo2(1)
+        project(0)
+
+        vec_rows_f32 = keep.tile([P, P], F32)
+        nc.vector.tensor_copy(out=vec_rows_f32[:], in_=vec_rows[:])
+        vec_cols_ps = psum_tr.tile([P, P], F32, tag="tr")
+        nc.tensor.transpose(vec_cols_ps[:], vec_rows_f32[:], ident[:])
+        vec_cols = keep.tile([P, 16], F32)
+        nc.vector.tensor_copy(out=vec_cols[:], in_=vec_cols_ps[:, 0:16])
+
+
+        for k in range(TILES + 2):
+            if 1 <= k <= TILES:
+                flip(k - 1)
+            if k + 1 < TILES:
+                project(k + 1)
+            if k < TILES:
+                residual(k)
+                add_bl(k)
+                statistics(k)
+            if k + 2 < TILES:
+                add_bo2(k + 2)
+            if 1 <= k <= TILES:
+                gain_and_bias(k - 1)
+            if k < TILES:
+                normalise(k)
+            if k == 0:
+                quantise_weight(nc, stage, wl_raw, wl_codes, wl_scales)
+            if 1 <= k <= TILES:
+                quantise_h(k - 1)
+                linear(k - 1)
+            if k >= 2:
+                finish(k - 2)

@@ -186,7 +186,7 @@ def tile_successiveswintransfomerblock_pb_kernel(tc, attn_win, x_mid, Wo2, bo2, 
 
         def add_bl(i):
             xbl[i] = stream.tile([P, D], F32, name="xbl")
-            nc.gpsimd.tensor_tensor(out=xbl[i][:], in0=x[i][:], in1=bl_all[:], op=ALU.add)
+            nc.vector.tensor_tensor(out=xbl[i][:], in0=x[i][:], in1=bl_all[:], op=ALU.add)
 
         def statistics(i):
             squares = short.tile([P, D], BF16)

@@ -151,7 +151,9 @@ def tile_successiveswintransfomerblock_pb_kernel(tc, attn_win, x_mid, Wo2, bo2, 
 
         def add_bo2(i):
             xb[i] = stream.tile([P, D], F32, name="xb")
-            nc.gpsimd.tensor_tensor(out=xb[i][:], in0=xmid_sb[:, i, :], in1=bo2_all[:], op=ALU.add)
+            for h in range(HALVES):
+                cols = slice(h * N_PASS, (h + 1) * N_PASS)
+                nc.gpsimd.tensor_tensor(out=xb[i][:, cols], in0=xmid_sb[:, i, cols], in1=bo2_all[:, cols], op=ALU.add)
 
         def project(i):
             toks = slice(i * P, (i + 1) * P)
@@ -186,7 +188,9 @@ def tile_successiveswintransfomerblock_pb_kernel(tc, attn_win, x_mid, Wo2, bo2, 
 
         def add_bl(i):
             xbl[i] = stream.tile([P, D], F32, name="xbl")
-            nc.vector.tensor_tensor(out=xbl[i][:], in0=x[i][:], in1=bl_all[:], op=ALU.add)
+            for h in range(HALVES):
+                cols = slice(h * N_PASS, (h + 1) * N_PASS)
+                nc.gpsimd.tensor_tensor(out=xbl[i][:, cols], in0=x[i][:, cols], in1=bl_all[:, cols], op=ALU.add)
 
         def statistics(i):
             squares = short.tile([P, D], BF16)

@@ -70,11 +70,13 @@ def tile_successiveswintransfomerblock_pb_kernel(tc, attn_win, x_mid, Wo2, bo2, 
     with ExitStack() as ctx:
         keep = ctx.enter_context(tc.tile_pool(name="keep", bufs=1))
         stage = ctx.enter_context(tc.tile_pool(name="stage", bufs=3))
-        stream = ctx.enter_context(tc.tile_pool(name="stream", bufs=3))
-        short = ctx.enter_context(tc.tile_pool(name="short", bufs=2))
-        small = ctx.enter_context(tc.tile_pool(name="small", bufs=4))
-        psum_mm = ctx.enter_context(tc.psum_pool(name="psum_mm", bufs=2))
-        psum_tr = ctx.enter_context(tc.psum_pool(name="psum_tr", bufs=4))
+        ahead = ctx.enter_context(tc.tile_pool(name="ahead", bufs=4))
+        rows_pool = ctx.enter_context(tc.tile_pool(name="rows_pool", bufs=7))
+        short = ctx.enter_context(tc.tile_pool(name="short", bufs=3))
+        small = ctx.enter_context(tc.tile_pool(name="small", bufs=8))
+        psum_acc1 = ctx.enter_context(tc.psum_pool(name="psum_acc1", bufs=4))
+        psum_acc2 = ctx.enter_context(tc.psum_pool(name="psum_acc2", bufs=2))
+        psum_tr = ctx.enter_context(tc.psum_pool(name="psum_tr", bufs=2))
 
         vec_rows = keep.tile([P, P], BF16)
         nc.vector.memset(vec_rows[:], 0.0)
@@ -99,12 +101,12 @@ def tile_successiveswintransfomerblock_pb_kernel(tc, attn_win, x_mid, Wo2, bo2, 
         wl_raw = keep.tile([P, PASSES * PACK, D], BF16)
         wl_src = Wl.rearrange("(c p) n -> p c n", p=P)
 
-        nc.sync.dma_start(out=attn_sb[:, 0:3, :], in_=attn_src[:, 0:3, :])
         for g in range(PASSES):
             nc.sync.dma_start(out=wo_dst[:, 2 * g : 2 * g + 2, :], in_=wo_src[:, 2 * g : 2 * g + 2, :])
+        nc.sync.dma_start(out=attn_sb[:, 0:3, :], in_=attn_src[:, 0:3, :])
+        nc.sync.dma_start(out=xmid_sb[:, 0:3, :], in_=xmid_src[:, 0:3, :])
         for first in range(3, TILES, 3):
             nc.sync.dma_start(out=attn_sb[:, first : first + 3, :], in_=attn_src[:, first : first + 3, :])
-        nc.sync.dma_start(out=xmid_sb[:, 0:3, :], in_=xmid_src[:, 0:3, :])
         for g in range(PASSES):
             nc.sync.dma_start(
                 out=wl_raw[:, g * PACK : (g + 1) * PACK, :], in_=wl_src[:, g * PACK : (g + 1) * PACK, :]
@@ -134,7 +136,7 @@ def tile_successiveswintransfomerblock_pb_kernel(tc, attn_win, x_mid, Wo2, bo2, 
                         for g in range(PASSES):
                             src = by_window[:, 2 * g : 2 * g + 2, w, i0 : i0 + n_rows, j0 : j0 + n_cols]
                             dst = by_patch[:, g, image, r0 : r0 + n_rows, c0 : c0 + n_cols, :]
-                            nc.scalar.copy(out=dst, in_=src.rearrange("p u i j -> p i j u"))
+                            nc.vector.tensor_copy(out=dst, in_=src.rearrange("p u i j -> p i j u"))
 
         def quantise_attn(i):
             toks = slice(i * P, (i + 1) * P)
@@ -145,21 +147,19 @@ def tile_successiveswintransfomerblock_pb_kernel(tc, attn_win, x_mid, Wo2, bo2, 
                     in_=attn_grouped[:, g, toks, :].rearrange("p n t -> p (n t)"),
                 )
 
-        xb, acc1, x, xbl, negmean, rstd, shift, xn, flipped_xn, planes, h_codes, h_scales, acc2 = (
-            {}, {}, {}, {}, {}, {}, {}, {}, {}, {}, {}, {}, {},
+        xb, acc1, x, negmean, rstd, shift, xn, flipped_xn, planes, h_codes, h_scales, acc2 = (
+            {}, {}, {}, {}, {}, {}, {}, {}, {}, {}, {}, {},
         )
 
         def add_bo2(i):
-            xb[i] = stream.tile([P, D], F32, name="xb")
-            for h in range(HALVES):
-                cols = slice(h * N_PASS, (h + 1) * N_PASS)
-                nc.gpsimd.tensor_tensor(out=xb[i][:, cols], in0=xmid_sb[:, i, cols], in1=bo2_all[:, cols], op=ALU.add)
+            xb[i] = ahead.tile([P, D], F32, name="xb")
+            nc.gpsimd.tensor_tensor(out=xb[i][:], in0=xmid_sb[:, i, :], in1=bo2_all[:], op=ALU.add)
 
         def project(i):
             toks = slice(i * P, (i + 1) * P)
             for h in range(HALVES):
                 cols = slice(h * N_PASS, (h + 1) * N_PASS)
-                acc1[i, h] = psum_mm.tile([P, N_PASS], F32, name="acc1")
+                acc1[i, h] = psum_acc1.tile([P, N_PASS], F32, name="acc1")
                 for g in range(PASSES):
                     nc.tensor.matmul_mx(
                         out=acc1[i, h][:],
@@ -172,7 +172,7 @@ def tile_successiveswintransfomerblock_pb_kernel(tc, attn_win, x_mid, Wo2, bo2, 
                     )
 
         def residual(i):
-            x[i] = stream.tile([P, D], F32, name="x")
+            x[i] = rows_pool.tile([P, D], F32, name="x")
             sums = small.tile([P, HALVES], F32)
             for h in range(HALVES):
                 cols = slice(h * N_PASS, (h + 1) * N_PASS)
@@ -187,10 +187,7 @@ def tile_successiveswintransfomerblock_pb_kernel(tc, attn_win, x_mid, Wo2, bo2, 
             )
 
         def add_bl(i):
-            xbl[i] = stream.tile([P, D], F32, name="xbl")
-            for h in range(HALVES):
-                cols = slice(h * N_PASS, (h + 1) * N_PASS)
-                nc.gpsimd.tensor_tensor(out=xbl[i][:, cols], in0=x[i][:, cols], in1=bl_all[:, cols], op=ALU.add)
+            nc.gpsimd.tensor_tensor(out=x[i][:], in0=x[i][:], in1=bl_all[:], op=ALU.add)
 
         def statistics(i):
             squares = short.tile([P, D], BF16)
@@ -241,7 +238,7 @@ def tile_successiveswintransfomerblock_pb_kernel(tc, attn_win, x_mid, Wo2, bo2, 
         def linear(i):
             for h in range(HALVES):
                 cols = slice(h * N_PASS, (h + 1) * N_PASS)
-                acc2[i, h] = psum_mm.tile([P, N_PASS], F32, name="acc2")
+                acc2[i, h] = psum_acc2.tile([P, N_PASS], F32, name="acc2")
                 for g in range(PASSES):
                     nc.tensor.matmul_mx(
                         out=acc2[i, h][:],
@@ -254,22 +251,25 @@ def tile_successiveswintransfomerblock_pb_kernel(tc, attn_win, x_mid, Wo2, bo2, 
                     )
 
         def finish(i):
-            result = stream.tile([P, D], F32)
             for h in range(HALVES):
                 cols = slice(h * N_PASS, (h + 1) * N_PASS)
-                nc.vector.tensor_tensor(out=result[:, cols], in0=acc2[i, h][:], in1=xbl[i][:, cols], op=ALU.add)
-            nc.sync.dma_start(out=out_rows[i * P : (i + 1) * P, :], in_=result[:])
+                nc.vector.tensor_tensor(out=x[i][:, cols], in0=acc2[i, h][:], in1=x[i][:, cols], op=ALU.add)
+            nc.sync.dma_start(out=out_rows[i * P : (i + 1) * P, :], in_=x[i][:])
 
+        quantise_weight(nc, stage, wo_raw, wo_codes, wo_scales)
         for s in range(3):
             flip_attn(s)
-        quantise_weight(nc, stage, wo_raw, wo_codes, wo_scales)
-        for s in range(3, TILES):
-            flip_attn(s)
-        for i in range(TILES):
-            quantise_attn(i)
-        add_bo2(0)
-        add_bo2(1)
+        quantise_attn(0)
+        quantise_attn(1)
+        for i in range(3):
+            add_bo2(i)
         project(0)
+        for s in range(3, 6):
+            flip_attn(s)
+        project(1)
+        quantise_attn(2)
+        for s in range(6, TILES):
+            flip_attn(s)
 
         vec_rows_f32 = keep.tile([P, P], F32)
         nc.vector.tensor_copy(out=vec_rows_f32[:], in_=vec_rows[:])
@@ -279,25 +279,27 @@ def tile_successiveswintransfomerblock_pb_kernel(tc, attn_win, x_mid, Wo2, bo2, 
         nc.vector.tensor_copy(out=vec_cols[:], in_=vec_cols_ps[:, 0:16])
 
 
-        for k in range(TILES + 2):
-            if 1 <= k <= TILES:
-                flip(k - 1)
-            if k + 1 < TILES:
-                project(k + 1)
+        for k in range(TILES + 5):
+            if 0 <= k - 4 < TILES:
+                finish(k - 4)
+            if 0 <= k - 2 < TILES:
+                flip(k - 2)
+            if 0 <= k - 3 < TILES:
+                quantise_h(k - 3)
+                linear(k - 3)
+            if 0 <= k - 1 < TILES:
+                statistics(k - 1)
+            if 0 <= k - 2 < TILES:
+                gain_and_bias(k - 2)
+                add_bl(k - 2)
+            if 0 <= k - 1 < TILES:
+                normalise(k - 1)
             if k < TILES:
                 residual(k)
-                add_bl(k)
-                statistics(k)
             if k + 2 < TILES:
-                add_bo2(k + 2)
-            if 1 <= k <= TILES:
-                gain_and_bias(k - 1)
-            if k < TILES:
-                normalise(k)
+                project(k + 2)
+            if k + 3 < TILES:
+                add_bo2(k + 3)
+                quantise_attn(k + 3)
             if k == 0:
                 quantise_weight(nc, stage, wl_raw, wl_codes, wl_scales)
-            if 1 <= k <= TILES:
-                quantise_h(k - 1)
-                linear(k - 1)
-            if k >= 2:
-                finish(k - 2)

@@ -39,26 +39,25 @@ def rolled_runs(w):
 V_COLS = 320
 
 
-def quantise_weight(nc, stage, raw, codes, scales):
-    for g in range(PASSES):
-        for h in range(HALVES):
-            first = h * N_PASS
-            grouped = stage.tile([P, N_PASS, PACK], BF16, align_bytes=64)
-            nc.vector.tensor_copy(
-                out=grouped[:, 0:V_COLS, :].rearrange("p (c i) t -> p c t i", i=4),
-                in_=raw[:, g * PACK : (g + 1) * PACK, first : first + V_COLS].rearrange("p t (c i) -> p c t i", i=4),
-            )
-            nc.scalar.copy(
-                out=grouped[:, V_COLS:N_PASS, :].rearrange("p (c i) t -> p c t i", i=4),
-                in_=raw[:, g * PACK : (g + 1) * PACK, first + V_COLS : first + N_PASS].rearrange(
-                    "p t (c i) -> p c t i", i=4
-                ),
-            )
-            nc.vector.quantize_mx(
-                out=codes[:, g, first : first + N_PASS].bitcast(FP8X4),
-                scales=scales[:, g, first : first + N_PASS],
-                in_=grouped[:].rearrange("p n t -> p (n t)"),
-            )
+def quantise_weight(nc, stage, raw, codes, scales, g):
+    for h in range(HALVES):
+        first = h * N_PASS
+        grouped = stage.tile([P, N_PASS, PACK], BF16, align_bytes=64)
+        nc.vector.tensor_copy(
+            out=grouped[:, 0:V_COLS, :].rearrange("p (c i) t -> p c t i", i=4),
+            in_=raw[:, g * PACK : (g + 1) * PACK, first : first + V_COLS].rearrange("p t (c i) -> p c t i", i=4),
+        )
+        nc.scalar.copy(
+            out=grouped[:, V_COLS:N_PASS, :].rearrange("p (c i) t -> p c t i", i=4),
+            in_=raw[:, g * PACK : (g + 1) * PACK, first + V_COLS : first + N_PASS].rearrange(
+                "p t (c i) -> p c t i", i=4
+            ),
+        )
+        nc.vector.quantize_mx(
+            out=codes[:, g, first : first + N_PASS].bitcast(FP8X4),
+            scales=scales[:, g, first : first + N_PASS],
+            in_=grouped[:].rearrange("p n t -> p (n t)"),
+        )
 
 
 def tile_successiveswintransfomerblock_pb_kernel(tc, attn_win, x_mid, Wo2, bo2, g4, b4, Wl, bl, out):
@@ -74,18 +73,21 @@ def tile_successiveswintransfomerblock_pb_kernel(tc, attn_win, x_mid, Wo2, bo2, 
         rows_pool = ctx.enter_context(tc.tile_pool(name="rows_pool", bufs=7))
         short = ctx.enter_context(tc.tile_pool(name="short", bufs=3))
         small = ctx.enter_context(tc.tile_pool(name="small", bufs=8))
-        psum_acc1 = ctx.enter_context(tc.psum_pool(name="psum_acc1", bufs=4))
-        psum_acc2 = ctx.enter_context(tc.psum_pool(name="psum_acc2", bufs=2))
+        psum_acc1 = ctx.enter_context(tc.psum_pool(name="psum_acc1", bufs=2))
+        psum_acc2 = ctx.enter_context(tc.psum_pool(name="psum_acc2", bufs=4))
         psum_tr = ctx.enter_context(tc.psum_pool(name="psum_tr", bufs=2))
+        ctx.enter_context(tc.manual_schedule())
 
         vec_rows = keep.tile([P, P], BF16)
         nc.vector.memset(vec_rows[:], 0.0)
-        nc.scalar.dma_start(out=vec_rows[0:8, :], in_=g4.rearrange("(c p) -> c p", p=P))
-        nc.scalar.dma_start(out=vec_rows[8:16, :], in_=b4.rearrange("(c p) -> c p", p=P))
-        bo2_all = keep.tile([P, D], BF16)
-        nc.scalar.dma_start(out=bo2_all[:], in_=bo2.partition_broadcast(P))
-        bl_all = keep.tile([P, D], BF16)
-        nc.scalar.dma_start(out=bl_all[:], in_=bl.partition_broadcast(P))
+        nc.sync.dma_start(out=vec_rows[0:8, :], in_=g4.rearrange("(c p) -> c p", p=P))
+        nc.sync.dma_start(out=vec_rows[8:16, :], in_=b4.rearrange("(c p) -> c p", p=P))
+        bias_rows = keep.tile([P, 2 * D], BF16)
+        nc.vector.memset(bias_rows[:], 0.0)
+        nc.sync.dma_start(out=bias_rows[0:1, 0:D], in_=bo2.rearrange("(o d) -> o d", o=1))
+        nc.sync.dma_start(out=bias_rows[0:1, D : 2 * D], in_=bl.rearrange("(o d) -> o d", o=1))
+        ones = keep.tile([P, P], BF16)
+        nc.vector.memset(ones[:], 1.0)
         eps = keep.tile([P, 1], F32)
         nc.vector.memset(eps[:], LN_EPS)
         ident = keep.tile([P, P], F32)
@@ -136,7 +138,7 @@ def tile_successiveswintransfomerblock_pb_kernel(tc, attn_win, x_mid, Wo2, bo2, 
                         for g in range(PASSES):
                             src = by_window[:, 2 * g : 2 * g + 2, w, i0 : i0 + n_rows, j0 : j0 + n_cols]
                             dst = by_patch[:, g, image, r0 : r0 + n_rows, c0 : c0 + n_cols, :]
-                            nc.vector.tensor_copy(out=dst, in_=src.rearrange("p u i j -> p i j u"))
+                            nc.scalar.copy(out=dst, in_=src.rearrange("p u i j -> p i j u"))
 
         def quantise_attn(i):
             toks = slice(i * P, (i + 1) * P)
@@ -153,7 +155,7 @@ def tile_successiveswintransfomerblock_pb_kernel(tc, attn_win, x_mid, Wo2, bo2, 
 
         def add_bo2(i):
             xb[i] = ahead.tile([P, D], F32, name="xb")
-            nc.gpsimd.tensor_tensor(out=xb[i][:], in0=xmid_sb[:, i, :], in1=bo2_all[:], op=ALU.add)
+            nc.gpsimd.tensor_tensor(out=xb[i][:], in0=xmid_sb[:, i, :], in1=bias_all[:, 0:D], op=ALU.add)
 
         def project(i):
             toks = slice(i * P, (i + 1) * P)
@@ -187,7 +189,7 @@ def tile_successiveswintransfomerblock_pb_kernel(tc, attn_win, x_mid, Wo2, bo2, 
             )
 
         def add_bl(i):
-            nc.gpsimd.tensor_tensor(out=x[i][:], in0=x[i][:], in1=bl_all[:], op=ALU.add)
+            nc.gpsimd.tensor_tensor(out=x[i][:], in0=x[i][:], in1=bias_all[:, D : 2 * D], op=ALU.add)
 
         def statistics(i):
             squares = short.tile([P, D], BF16)
@@ -213,14 +215,9 @@ def tile_successiveswintransfomerblock_pb_kernel(tc, attn_win, x_mid, Wo2, bo2, 
 
         def gain_and_bias(i):
             planes[i] = short.tile([P, PASSES * PACK, P], BF16, name="planes")
-            for t in range(PACK):
-                nc.vector.tensor_scalar(
-                    out=planes[i][:, t, :], in0=flipped_xn[i, 0][:, t, :],
-                    scalar1=vec_cols[:, t : t + 1], scalar2=vec_cols[:, 8 + t : 9 + t], op0=ALU.mult, op1=ALU.add,
-                )
-                c = PACK + t
+            for c in range(PASSES * PACK):
                 nc.scalar.activation(
-                    out=planes[i][:, c, :], in_=flipped_xn[i, 1][:, t, :], func=ACT.Identity,
+                    out=planes[i][:, c, :], in_=flipped_xn[i, c // PACK][:, c % PACK, :], func=ACT.Identity,
                     bias=vec_cols[:, 8 + c : 9 + c], scale=vec_cols[:, c : c + 1],
                 )
 
@@ -256,7 +253,22 @@ def tile_successiveswintransfomerblock_pb_kernel(tc, attn_win, x_mid, Wo2, bo2, 
                 nc.vector.tensor_tensor(out=x[i][:, cols], in0=acc2[i, h][:], in1=x[i][:, cols], op=ALU.add)
             nc.sync.dma_start(out=out_rows[i * P : (i + 1) * P, :], in_=x[i][:])
 
-        quantise_weight(nc, stage, wo_raw, wo_codes, wo_scales)
+        bias_all = keep.tile([P, 2 * D], BF16)
+        for j in range(2 * HALVES):
+            cols = slice(j * N_PASS, (j + 1) * N_PASS)
+            spread = psum_tr.tile([P, N_PASS], F32, tag="tr")
+            nc.tensor.matmul(out=spread[:], lhsT=ones[:], rhs=bias_rows[:, cols], start=True, stop=True)
+            nc.scalar.copy(out=bias_all[:, cols], in_=spread[:])
+        vec_rows_f32 = keep.tile([P, P], F32)
+        nc.vector.tensor_copy(out=vec_rows_f32[:], in_=vec_rows[:])
+        vec_cols_ps = psum_tr.tile([P, P], F32, tag="tr")
+        nc.tensor.transpose(vec_cols_ps[:], vec_rows_f32[:], ident[:])
+        vec_cols = keep.tile([P, 16], F32)
+        nc.vector.tensor_copy(out=vec_cols[:], in_=vec_cols_ps[:, 0:16])
+
+
+        for g in range(PASSES):
+            quantise_weight(nc, stage, wo_raw, wo_codes, wo_scales, g)
         for s in range(3):
             flip_attn(s)
         quantise_attn(0)
@@ -266,40 +278,34 @@ def tile_successiveswintransfomerblock_pb_kernel(tc, attn_win, x_mid, Wo2, bo2, 
         project(0)
         for s in range(3, 6):
             flip_attn(s)
-        project(1)
         quantise_attn(2)
         for s in range(6, TILES):
             flip_attn(s)
 
-        vec_rows_f32 = keep.tile([P, P], F32)
-        nc.vector.tensor_copy(out=vec_rows_f32[:], in_=vec_rows[:])
-        vec_cols_ps = psum_tr.tile([P, P], F32, tag="tr")
-        nc.tensor.transpose(vec_cols_ps[:], vec_rows_f32[:], ident[:])
-        vec_cols = keep.tile([P, 16], F32)
-        nc.vector.tensor_copy(out=vec_cols[:], in_=vec_cols_ps[:, 0:16])
-
-
         for k in range(TILES + 5):
-            if 0 <= k - 4 < TILES:
-                finish(k - 4)
             if 0 <= k - 2 < TILES:
                 flip(k - 2)
             if 0 <= k - 3 < TILES:
-                quantise_h(k - 3)
                 linear(k - 3)
+            if k < TILES:
+                residual(k)
+            if k + 1 < TILES:
+                project(k + 1)
+            if 0 <= k - 2 < TILES:
+                add_bl(k - 2)
+            if k + 3 < TILES:
+                add_bo2(k + 3)
             if 0 <= k - 1 < TILES:
                 statistics(k - 1)
             if 0 <= k - 2 < TILES:
                 gain_and_bias(k - 2)
-                add_bl(k - 2)
             if 0 <= k - 1 < TILES:
                 normalise(k - 1)
-            if k < TILES:
-                residual(k)
-            if k + 2 < TILES:
-                project(k + 2)
+            if k < PASSES:
+                quantise_weight(nc, stage, wl_raw, wl_codes, wl_scales, k)
+            if 0 <= k - 4 < TILES:
+                finish(k - 4)
+            if 0 <= k - 2 < TILES:
+                quantise_h(k - 2)
             if k + 3 < TILES:
-                add_bo2(k + 3)
                 quantise_attn(k + 3)
-            if k == 0:
-                quantise_weight(nc, stage, wl_raw, wl_codes, wl_scales)

@@ -36,6 +36,7 @@ def rolled_runs(w):
     return [(0, WS, start)]
 
 
+EARLY_ATTN = 5
 V_COLS = 320
 
 
@@ -70,7 +71,7 @@ def tile_successiveswintransfomerblock_pb_kernel(tc, attn_win, x_mid, Wo2, bo2, 
         keep = ctx.enter_context(tc.tile_pool(name="keep", bufs=1))
         stage = ctx.enter_context(tc.tile_pool(name="stage", bufs=3))
         ahead = ctx.enter_context(tc.tile_pool(name="ahead", bufs=4))
-        rows_pool = ctx.enter_context(tc.tile_pool(name="rows_pool", bufs=7))
+        rows_pool = ctx.enter_context(tc.tile_pool(name="rows_pool", bufs=8))
         short = ctx.enter_context(tc.tile_pool(name="short", bufs=3))
         small = ctx.enter_context(tc.tile_pool(name="small", bufs=8))
         psum_acc1 = ctx.enter_context(tc.psum_pool(name="psum_acc1", bufs=2))
@@ -126,7 +127,7 @@ def tile_successiveswintransfomerblock_pb_kernel(tc, attn_win, x_mid, Wo2, bo2, 
         by_patch = attn_grouped[:].bitcast(F32).rearrange("p g (b r c) u -> p g b r c u", r=SIDE, c=SIDE)
 
         def flip_attn(s):
-            flipped = psum_tr.tile([P, PASSES * 2, P], F32, tag="tr")
+            flipped = psum_acc2.tile([P, PASSES * 2, P], F32, tag="acc2")
             for c in range(PASSES * 2):
                 nc.tensor.transpose(flipped[:, c, :], attn_sb[:, s, :].bitcast(F32)[:, c * P : (c + 1) * P], ident[:])
             by_window = flipped[:].rearrange("p c (w i j) -> p c w i j", i=WS, j=WS)
@@ -276,36 +277,34 @@ def tile_successiveswintransfomerblock_pb_kernel(tc, attn_win, x_mid, Wo2, bo2, 
         for i in range(3):
             add_bo2(i)
         project(0)
-        for s in range(3, 6):
+        for s in range(3, EARLY_ATTN):
             flip_attn(s)
         quantise_attn(2)
-        for s in range(6, TILES):
-            flip_attn(s)
 
         for k in range(TILES + 5):
             if 0 <= k - 2 < TILES:
                 flip(k - 2)
-            if 0 <= k - 3 < TILES:
-                linear(k - 3)
-            if k < TILES:
-                residual(k)
-            if k + 1 < TILES:
-                project(k + 1)
-            if 0 <= k - 2 < TILES:
-                add_bl(k - 2)
-            if k + 3 < TILES:
-                add_bo2(k + 3)
             if 0 <= k - 1 < TILES:
                 statistics(k - 1)
-            if 0 <= k - 2 < TILES:
-                gain_and_bias(k - 2)
-            if 0 <= k - 1 < TILES:
-                normalise(k - 1)
+            if k < TILES:
+                residual(k)
             if k < PASSES:
                 quantise_weight(nc, stage, wl_raw, wl_codes, wl_scales, k)
+            if 0 <= k - 1 < TILES:
+                normalise(k - 1)
+            if 0 <= k - 2 < TILES:
+                gain_and_bias(k - 2)
+                add_bl(k - 2)
+            if EARLY_ATTN + k < TILES:
+                flip_attn(EARLY_ATTN + k)
             if 0 <= k - 4 < TILES:
                 finish(k - 4)
+            if 0 <= k - 3 < TILES:
+                linear(k - 3)
+            if k + 1 < TILES:
+                project(k + 1)
             if 0 <= k - 2 < TILES:
                 quantise_h(k - 2)
             if k + 3 < TILES:
                 quantise_attn(k + 3)
+                add_bo2(k + 3)

@@ -190,7 +190,7 @@ def tile_successiveswintransfomerblock_pb_kernel(tc, attn_win, x_mid, Wo2, bo2, 
             )
 
         def add_bl(i):
-            nc.gpsimd.tensor_tensor(out=x[i][:], in0=x[i][:], in1=bias_all[:, D : 2 * D], op=ALU.add)
+            nc.vector.tensor_tensor(out=x[i][:], in0=x[i][:], in1=bias_all[:, D : 2 * D], op=ALU.add)
 
         def statistics(i):
             squares = short.tile([P, D], BF16)
@@ -294,11 +294,12 @@ def tile_successiveswintransfomerblock_pb_kernel(tc, attn_win, x_mid, Wo2, bo2, 
                 normalise(k - 1)
             if 0 <= k - 2 < TILES:
                 gain_and_bias(k - 2)
-                add_bl(k - 2)
             if EARLY_ATTN + k < TILES:
                 flip_attn(EARLY_ATTN + k)
             if 0 <= k - 4 < TILES:
                 finish(k - 4)
+            if 0 <= k - 2 < TILES:
+                add_bl(k - 2)
             if 0 <= k - 3 < TILES:
                 linear(k - 3)
             if k + 1 < TILES:

@@ -150,8 +150,8 @@ def tile_successiveswintransfomerblock_pb_kernel(tc, attn_win, x_mid, Wo2, bo2, 
                     in_=attn_grouped[:, g, toks, :].rearrange("p n t -> p (n t)"),
                 )
 
-        xb, acc1, x, negmean, rstd, shift, xn, flipped_xn, planes, h_codes, h_scales, acc2 = (
-            {}, {}, {}, {}, {}, {}, {}, {}, {}, {}, {}, {},
+        xb, acc1, x, negmean, rstd, xn, flipped_xn, planes, h_codes, h_scales, acc2 = (
+            {}, {}, {}, {}, {}, {}, {}, {}, {}, {}, {},
         )
 
         def add_bo2(i):
@@ -190,7 +190,7 @@ def tile_successiveswintransfomerblock_pb_kernel(tc, attn_win, x_mid, Wo2, bo2, 
             )
 
         def add_bl(i):
-            nc.vector.tensor_tensor(out=x[i][:], in0=x[i][:], in1=bias_all[:, D : 2 * D], op=ALU.add)
+            nc.gpsimd.tensor_tensor(out=x[i][:], in0=x[i][:], in1=bias_all[:, D : 2 * D], op=ALU.add)
 
         def statistics(i):
             squares = short.tile([P, D], BF16)
@@ -200,12 +200,12 @@ def tile_successiveswintransfomerblock_pb_kernel(tc, attn_win, x_mid, Wo2, bo2, 
             )
             rstd[i] = small.tile([P, 1], F32, name="rstd")
             nc.scalar.activation(out=rstd[i][:], in_=ssq[:], func=ACT.Abs_reciprocal_sqrt, bias=eps[:], scale=1.0 / D)
-            shift[i] = small.tile([P, 1], F32, name="shift")
-            nc.scalar.activation(out=shift[i][:], in_=negmean[i][:], func=ACT.Identity, scale=rstd[i][:])
 
         def normalise(i):
             xn[i] = short.tile([P, D], F32, name="xn")
-            nc.scalar.activation(out=xn[i][:], in_=x[i][:], func=ACT.Identity, bias=shift[i][:], scale=rstd[i][:])
+            nc.vector.tensor_scalar(
+                out=xn[i][:], in0=x[i][:], scalar1=negmean[i][:], scalar2=rstd[i][:], op0=ALU.add, op1=ALU.mult
+            )
 
         def flip(i):
             for g in range(PASSES):
@@ -290,16 +290,15 @@ def tile_successiveswintransfomerblock_pb_kernel(tc, attn_win, x_mid, Wo2, bo2, 
                 residual(k)
             if k < PASSES:
                 quantise_weight(nc, stage, wl_raw, wl_codes, wl_scales, k)
-            if 0 <= k - 1 < TILES:
-                normalise(k - 1)
             if 0 <= k - 2 < TILES:
                 gain_and_bias(k - 2)
+                add_bl(k - 2)
             if EARLY_ATTN + k < TILES:
                 flip_attn(EARLY_ATTN + k)
             if 0 <= k - 4 < TILES:
                 finish(k - 4)
-            if 0 <= k - 2 < TILES:
-                add_bl(k - 2)
+            if 0 <= k - 1 < TILES:
+                normalise(k - 1)
             if 0 <= k - 3 < TILES:
                 linear(k - 3)
             if k + 1 < TILES:

from contextlib import ExitStack

import concourse.mybir as mybir
from concourse.masks import make_identity

F32 = mybir.dt.float32
BF16 = mybir.dt.bfloat16
U32 = mybir.dt.uint32
U8 = mybir.dt.uint8
FP8X4 = mybir.dt.float8_e4m3fn_x4
ALU = mybir.AluOpType
ACT = mybir.ActivationFunctionType

P = 128
D = 1024
PACK = 4
K_PASS = P * PACK
PASSES = D // K_PASS
N_PASS = 512
HALVES = D // N_PASS
IMAGES = 2
SIDE = 24
WS = 8
WN = SIDE // WS
SHIFT = WS // 2
TOKENS = IMAGES * SIDE * SIDE
TILES = TOKENS // P
LN_EPS = 1e-5
FLOPS = 2 * 2 * TOKENS * D * D


def rolled_runs(w):
    start = WS * w - SHIFT
    if start < 0:
        return [(0, SHIFT, start + SIDE), (SHIFT, WS - SHIFT, 0)]
    return [(0, WS, start)]


EARLY_ATTN = 5
V_COLS = 320


def quantise_weight(nc, stage, raw, codes, scales, g):
    for h in range(HALVES):
        first = h * N_PASS
        grouped = stage.tile([P, N_PASS, PACK], BF16, align_bytes=64)
        nc.vector.tensor_copy(
            out=grouped[:, 0:V_COLS, :].rearrange("p (c i) t -> p c t i", i=4),
            in_=raw[:, g * PACK : (g + 1) * PACK, first : first + V_COLS].rearrange("p t (c i) -> p c t i", i=4),
        )
        nc.scalar.copy(
            out=grouped[:, V_COLS:N_PASS, :].rearrange("p (c i) t -> p c t i", i=4),
            in_=raw[:, g * PACK : (g + 1) * PACK, first + V_COLS : first + N_PASS].rearrange(
                "p t (c i) -> p c t i", i=4
            ),
        )
        nc.vector.quantize_mx(
            out=codes[:, g, first : first + N_PASS].bitcast(FP8X4),
            scales=scales[:, g, first : first + N_PASS],
            in_=grouped[:].rearrange("p n t -> p (n t)"),
        )


def tile_successiveswintransfomerblock_pb_kernel(tc, attn_win, x_mid, Wo2, bo2, g4, b4, Wl, bl, out):
    nc = tc.nc
    attn_rows = attn_win.flatten_outer_dims()
    xmid_rows = x_mid.flatten_outer_dims()
    out_rows = out.flatten_outer_dims()

    with ExitStack() as ctx:
        keep = ctx.enter_context(tc.tile_pool(name="keep", bufs=1))
        stage = ctx.enter_context(tc.tile_pool(name="stage", bufs=3))
        ahead = ctx.enter_context(tc.tile_pool(name="ahead", bufs=4))
        rows_pool = ctx.enter_context(tc.tile_pool(name="rows_pool", bufs=8))
        short = ctx.enter_context(tc.tile_pool(name="short", bufs=3))
        small = ctx.enter_context(tc.tile_pool(name="small", bufs=8))
        psum_acc1 = ctx.enter_context(tc.psum_pool(name="psum_acc1", bufs=2))
        psum_acc2 = ctx.enter_context(tc.psum_pool(name="psum_acc2", bufs=4))
        psum_tr = ctx.enter_context(tc.psum_pool(name="psum_tr", bufs=2))
        ctx.enter_context(tc.manual_schedule())

        vec_rows = keep.tile([P, P], BF16)
        nc.vector.memset(vec_rows[:], 0.0)
        nc.sync.dma_start(out=vec_rows[0:8, :], in_=g4.rearrange("(c p) -> c p", p=P))
        nc.sync.dma_start(out=vec_rows[8:16, :], in_=b4.rearrange("(c p) -> c p", p=P))
        bias_rows = keep.tile([P, 2 * D], BF16)
        nc.vector.memset(bias_rows[:], 0.0)
        nc.sync.dma_start(out=bias_rows[0:1, 0:D], in_=bo2.rearrange("(o d) -> o d", o=1))
        nc.sync.dma_start(out=bias_rows[0:1, D : 2 * D], in_=bl.rearrange("(o d) -> o d", o=1))
        ones = keep.tile([P, P], BF16)
        nc.vector.memset(ones[:], 1.0)
        eps = keep.tile([P, 1], F32)
        nc.vector.memset(eps[:], LN_EPS)
        ident = keep.tile([P, P], F32)
        make_identity(nc, ident[:])

        attn_sb = keep.tile([P, TILES, D], BF16)
        attn_src = attn_rows.rearrange("(s q) d -> q s d", q=P)
        xmid_sb = keep.tile([P, TILES, D], BF16)
        xmid_src = xmid_rows.rearrange("(s q) d -> q s d", q=P)
        wo_raw = keep.tile([P, PASSES * PACK, D], BF16)
        wo_dst = wo_raw[:].rearrange("q (c e) n -> q c (e n)", e=2)
        wo_src = Wo2.rearrange("(c q e) n -> q c (e n)", q=P, e=2)
        wl_raw = keep.tile([P, PASSES * PACK, D], BF16)
        wl_src = Wl.rearrange("(c p) n -> p c n", p=P)

        for g in range(PASSES):
            nc.sync.dma_start(out=wo_dst[:, 2 * g : 2 * g + 2, :], in_=wo_src[:, 2 * g : 2 * g + 2, :])
        nc.sync.dma_start(out=attn_sb[:, 0:3, :], in_=attn_src[:, 0:3, :])
        nc.sync.dma_start(out=xmid_sb[:, 0:3, :], in_=xmid_src[:, 0:3, :])
        for first in range(3, TILES, 3):
            nc.sync.dma_start(out=attn_sb[:, first : first + 3, :], in_=attn_src[:, first : first + 3, :])
        for g in range(PASSES):
            nc.sync.dma_start(
                out=wl_raw[:, g * PACK : (g + 1) * PACK, :], in_=wl_src[:, g * PACK : (g + 1) * PACK, :]
            )
        for first in range(3, TILES, 3):
            nc.sync.dma_start(out=xmid_sb[:, first : first + 3, :], in_=xmid_src[:, first : first + 3, :])

        wo_codes = keep.tile([P, PASSES, D], U32, align_bytes=64)
        wo_scales = keep.tile([P, PASSES, D], U8, align_bytes=64)
        wl_codes = keep.tile([P, PASSES, D], U32, align_bytes=64)
        wl_scales = keep.tile([P, PASSES, D], U8, align_bytes=64)
        attn_grouped = keep.tile([P, PASSES, TOKENS, PACK], BF16, align_bytes=64)
        attn_codes = keep.tile([P, PASSES, TOKENS], U32, align_bytes=64)
        attn_scales = keep.tile([P, PASSES, TOKENS], U8, align_bytes=64)
        by_patch = attn_grouped[:].bitcast(F32).rearrange("p g (b r c) u -> p g b r c u", r=SIDE, c=SIDE)

        def flip_attn(s):
            flipped = psum_acc2.tile([P, PASSES * 2, P], F32, tag="acc2")
            for c in range(PASSES * 2):
                nc.tensor.transpose(flipped[:, c, :], attn_sb[:, s, :].bitcast(F32)[:, c * P : (c + 1) * P], ident[:])
            by_window = flipped[:].rearrange("p c (w i j) -> p c w i j", i=WS, j=WS)
            for w in range(2):
                image, in_image = divmod(2 * s + w, WN * WN)
                wr, wc = divmod(in_image, WN)
                for i0, n_rows, r0 in rolled_runs(wr):
                    for j0, n_cols, c0 in rolled_runs(wc):
                        for g in range(PASSES):
                            src = by_window[:, 2 * g : 2 * g + 2, w, i0 : i0 + n_rows, j0 : j0 + n_cols]
                            dst = by_patch[:, g, image, r0 : r0 + n_rows, c0 : c0 + n_cols, :]
                            nc.scalar.copy(out=dst, in_=src.rearrange("p u i j -> p i j u"))

        def quantise_attn(i):
            toks = slice(i * P, (i + 1) * P)
            for g in range(PASSES):
                nc.vector.quantize_mx(
                    out=attn_codes[:, g, toks].bitcast(FP8X4),
                    scales=attn_scales[:, g, toks],
                    in_=attn_grouped[:, g, toks, :].rearrange("p n t -> p (n t)"),
                )

        xb, acc1, x, negmean, rstd, xn, flipped_xn, planes, h_codes, h_scales, acc2 = (
            {}, {}, {}, {}, {}, {}, {}, {}, {}, {}, {},
        )

        def add_bo2(i):
            xb[i] = ahead.tile([P, D], F32, name="xb")
            nc.gpsimd.tensor_tensor(out=xb[i][:], in0=xmid_sb[:, i, :], in1=bias_all[:, 0:D], op=ALU.add)

        def project(i):
            toks = slice(i * P, (i + 1) * P)
            for h in range(HALVES):
                cols = slice(h * N_PASS, (h + 1) * N_PASS)
                acc1[i, h] = psum_acc1.tile([P, N_PASS], F32, name="acc1")
                for g in range(PASSES):
                    nc.tensor.matmul_mx(
                        out=acc1[i, h][:],
                        lhsT=attn_codes[:, g, toks].bitcast(FP8X4),
                        lhsT_scale=attn_scales[:, g, toks],
                        rhs=wo_codes[:, g, cols].bitcast(FP8X4),
                        rhs_scale=wo_scales[:, g, cols],
                        start=(g == 0),
                        stop=(g == PASSES - 1),
                    )

        def residual(i):
            x[i] = rows_pool.tile([P, D], F32, name="x")
            sums = small.tile([P, HALVES], F32)
            for h in range(HALVES):
                cols = slice(h * N_PASS, (h + 1) * N_PASS)
                nc.vector.scalar_tensor_tensor(
                    out=x[i][:, cols], in0=acc1[i, h][:], scalar=1.0, in1=xb[i][:, cols],
                    op0=ALU.mult, op1=ALU.add, accum_out=sums[:, h : h + 1],
                )
            negmean[i] = small.tile([P, 1], F32, name="negmean")
            nc.vector.tensor_scalar(
                out=negmean[i][:], in0=sums[:, 0:1], scalar1=sums[:, 1:2], scalar2=-1.0 / D,
                op0=ALU.add, op1=ALU.mult,
            )

        def add_bl(i):
            nc.gpsimd.tensor_tensor(out=x[i][:], in0=x[i][:], in1=bias_all[:, D : 2 * D], op=ALU.add)

        def statistics(i):
            squares = short.tile([P, D], BF16)
            ssq = small.tile([P, 1], F32)
            nc.scalar.activation(
                out=squares[:], in_=x[i][:], func=ACT.Square, bias=negmean[i][:], scale=1.0, accum_out=ssq[:]
            )
            rstd[i] = small.tile([P, 1], F32, name="rstd")
            nc.scalar.activation(out=rstd[i][:], in_=ssq[:], func=ACT.Abs_reciprocal_sqrt, bias=eps[:], scale=1.0 / D)

        def normalise(i):
            xn[i] = short.tile([P, D], F32, name="xn")
            nc.vector.tensor_scalar(
                out=xn[i][:], in0=x[i][:], scalar1=negmean[i][:], scalar2=rstd[i][:], op0=ALU.add, op1=ALU.mult
            )

        def flip(i):
            for g in range(PASSES):
                flipped_xn[i, g] = psum_tr.tile([P, PACK, P], F32, name="flipped_xn", tag="tr")
                for t in range(PACK):
                    c = g * PACK + t
                    nc.tensor.transpose(flipped_xn[i, g][:, t, :], xn[i][:, c * P : (c + 1) * P], ident[:])

        def gain_and_bias(i):
            planes[i] = short.tile([P, PASSES * PACK, P], BF16, name="planes")
            for c in range(PASSES * PACK):
                nc.scalar.activation(
                    out=planes[i][:, c, :], in_=flipped_xn[i, c // PACK][:, c % PACK, :], func=ACT.Identity,
                    bias=vec_cols[:, 8 + c : 9 + c], scale=vec_cols[:, c : c + 1],
                )

        def quantise_h(i):
            h_grouped = short.tile([P, PASSES, P, PACK], BF16, align_bytes=64)
            nc.vector.tensor_copy(out=h_grouped[:], in_=planes[i][:].rearrange("p (g t) n -> p g n t", t=PACK))
            h_codes[i] = short.tile([P, PASSES, P], U32, align_bytes=64, name="h_codes")
            h_scales[i] = short.tile([P, PASSES, P], U8, align_bytes=64, name="h_scales")
            nc.vector.quantize_mx(
                out=h_codes[i][:].rearrange("p g n -> p (g n)").bitcast(FP8X4),
                scales=h_scales[i][:].rearrange("p g n -> p (g n)"),
                in_=h_grouped[:].rearrange("p g n t -> p (g n t)"),
            )

        def linear(i):
            for h in range(HALVES):
                cols = slice(h * N_PASS, (h + 1) * N_PASS)
                acc2[i, h] = psum_acc2.tile([P, N_PASS], F32, name="acc2")
                for g in range(PASSES):
                    nc.tensor.matmul_mx(
                        out=acc2[i, h][:],
                        lhsT=h_codes[i][:, g, :].bitcast(FP8X4),
                        lhsT_scale=h_scales[i][:, g, :],
                        rhs=wl_codes[:, g, cols].bitcast(FP8X4),
                        rhs_scale=wl_scales[:, g, cols],
                        start=(g == 0),
                        stop=(g == PASSES - 1),
                    )

        def finish(i):
            for h in range(HALVES):
                cols = slice(h * N_PASS, (h + 1) * N_PASS)
                nc.vector.tensor_tensor(out=x[i][:, cols], in0=acc2[i, h][:], in1=x[i][:, cols], op=ALU.add)
            nc.sync.dma_start(out=out_rows[i * P : (i + 1) * P, :], in_=x[i][:])

        bias_all = keep.tile([P, 2 * D], BF16)
        for j in range(2 * HALVES):
            cols = slice(j * N_PASS, (j + 1) * N_PASS)
            spread = psum_tr.tile([P, N_PASS], F32, tag="tr")
            nc.tensor.matmul(out=spread[:], lhsT=ones[:], rhs=bias_rows[:, cols], start=True, stop=True)
            nc.scalar.copy(out=bias_all[:, cols], in_=spread[:])
        vec_rows_f32 = keep.tile([P, P], F32)
        nc.vector.tensor_copy(out=vec_rows_f32[:], in_=vec_rows[:])
        vec_cols_ps = psum_tr.tile([P, P], F32, tag="tr")
        nc.tensor.transpose(vec_cols_ps[:], vec_rows_f32[:], ident[:])
        vec_cols = keep.tile([P, 16], F32)
        nc.vector.tensor_copy(out=vec_cols[:], in_=vec_cols_ps[:, 0:16])


        for g in range(PASSES):
            quantise_weight(nc, stage, wo_raw, wo_codes, wo_scales, g)
        for s in range(3):
            flip_attn(s)
        quantise_attn(0)
        quantise_attn(1)
        for i in range(3):
            add_bo2(i)
        project(0)
        for s in range(3, EARLY_ATTN):
            flip_attn(s)
        quantise_attn(2)

        for k in range(TILES + 5):
            if 0 <= k - 2 < TILES:
                flip(k - 2)
            if 0 <= k - 1 < TILES:
                statistics(k - 1)
            if k < TILES:
                residual(k)
            if k < PASSES:
                quantise_weight(nc, stage, wl_raw, wl_codes, wl_scales, k)
            if 0 <= k - 2 < TILES:
                gain_and_bias(k - 2)
                add_bl(k - 2)
            if EARLY_ATTN + k < TILES:
                flip_attn(EARLY_ATTN + k)
            if 0 <= k - 4 < TILES:
                finish(k - 4)
            if 0 <= k - 1 < TILES:
                normalise(k - 1)
            if 0 <= k - 3 < TILES:
                linear(k - 3)
            if k + 1 < TILES:
                project(k + 1)
            if 0 <= k - 2 < TILES:
                quantise_h(k - 2)
            if k + 3 < TILES:
                quantise_attn(k + 3)
                add_bo2(k + 3)
